import numpy as np
import ml_dtypes


def mxq(x, axis, fmt="e4m3"):
    dtype, down = {"e4m3": (ml_dtypes.float8_e4m3fn, 7), "e5m2": (ml_dtypes.float8_e5m2, 14)}[fmt]
    v = np.moveaxis(np.asarray(x, np.float32).astype(ml_dtypes.bfloat16).astype(np.float64), axis, -1)
    blocks = v.reshape(v.shape[:-1] + (-1, 32))
    amax = np.abs(blocks).max(-1, keepdims=True)
    byte = np.maximum(np.where(amax > 0, np.frexp(amax)[1] - 1 + 127, 0) - down, 1)
    scale = np.exp2(byte - 127.0)
    codes = (blocks / scale).astype(np.float32).astype(dtype).astype(np.float64)
    return np.moveaxis((codes * scale).reshape(v.shape), -1, axis)


WIDE = False


def mx_kscale(k):
    if not WIDE:
        return np.ones(k)
    levels = np.array([10, -10, 5, -5, 0])
    a = np.random.permutation(np.resize(levels, k // 512 * 4)).reshape(k // 512, 4)
    idx = np.arange(k)
    return np.exp2(a[idx // 512, idx % 128 // 32])


BF16 = ml_dtypes.bfloat16


def bf(x):
    return np.asarray(x, np.float32).astype(BF16)


def f64(x):
    return np.asarray(x).astype(np.float64)


B, T, D, H = 8, 128, 1024, 1024


def sigmoid(v):
    return 1.0 / (1.0 + np.exp(-v))


def setup_inputs():
    s = mx_kscale(D)
    return {"x": bf(np.random.standard_normal((B, T, D)) * s),
            "Wq": bf(np.random.standard_normal((H, D)) * 1.0 / np.sqrt(D) / s),
            "bq": bf(np.random.standard_normal(H) * 0.5),
            "Wk": bf(np.random.standard_normal((H, D)) * 0.6 / np.sqrt(D) / s),
            "bk": bf(np.random.standard_normal(H) * 0.3),
            "Wv": bf(np.random.standard_normal((H, D)) * 2.0 / np.sqrt(D) / s),
            "bv": bf(np.random.standard_normal(H) * 0.5),
            "wbias": bf(np.random.uniform(0.0, 1.0, H))}


def reference(x, Wq, bq, Wk, bk, Wv, bv, wbias):
    xq = mxq(f64(x), 2, "e4m3")
    Q = (xq @ mxq(f64(Wq), 1, "e4m3").T) + f64(bq)
    K = (xq @ mxq(f64(Wk), 1, "e4m3").T) + f64(bk)
    V = (xq @ mxq(f64(Wv), 1, "e4m3").T) + f64(bv)
    Q_sig = sigmoid(Q)
    numer = np.exp(K + f64(wbias))
    denom = numer.sum(axis=0)
    weighted = (numer * V).sum(axis=0) / denom
    Yt = Q_sig * weighted
    return Yt

@@ -1,0 +1,284 @@
+from contextlib import ExitStack
+
+import concourse.mybir as mybir
+from concourse.masks import make_identity
+
+FLOPS = 2 * 1024 * 1024 * 3072
+
+F32 = mybir.dt.float32
+BF16 = mybir.dt.bfloat16
+U32 = mybir.dt.uint32
+U8 = mybir.dt.uint8
+FP8X4 = mybir.dt.float8_e4m3fn_x4
+ACT = mybir.ActivationFunctionType
+ALU = mybir.AluOpType
+
+P = 128
+B = 8
+D = 1024
+H = 1024
+CH = 256
+NCH = H // CH
+PINNED = True
+PSUM_ON_G = True
+
+
+def tile_aftattention_kernel(tc, x, Wq, bq, Wk, bk, Wv, bv, wbias, out):
+    nc = tc.nc
+    with ExitStack() as ctx:
+        const = ctx.enter_context(tc.tile_pool(name="const", bufs=1))
+        gwp = ctx.enter_context(tc.tile_pool(name="gwp", bufs=4))
+        nump = ctx.enter_context(tc.tile_pool(name="nump", bufs=6))
+        prodp = ctx.enter_context(tc.tile_pool(name="prodp", bufs=6))
+        accp = ctx.enter_context(tc.tile_pool(name="accp", bufs=2))
+        thp = ctx.enter_context(tc.tile_pool(name="thp", bufs=8))
+        outp = ctx.enter_context(tc.tile_pool(name="outp", bufs=4))
+        trp = ctx.enter_context(tc.psum_pool(name="trp", bufs=3))
+        mxp = ctx.enter_context(tc.psum_pool(name="mxp", bufs=3))
+        otp = ctx.enter_context(tc.psum_pool(name="otp", bufs=2))
+        if PINNED:
+            ctx.enter_context(tc.manual_schedule())
+
+        ident = const.tile([P, P], F32, name="ident")
+        make_identity(nc, ident[:])
+        identb = const.tile([P, P], BF16, name="identb")
+        brow = const.tile([P, P], BF16, name="brow")
+        bvrow = const.tile([P, H], BF16, name="bvrow")
+        halves = const.tile([P, P], BF16, name="halves")
+        warm = const.tile([P, 1], F32, name="warm")
+        warm2 = const.tile([P, 1], F32, name="warm2")
+        bqh = const.tile([P, 8], F32, name="bqh")
+        bvh = const.tile([P, H], F32, name="bvh")
+        nc.vector.memset(warm[:], 0.0)
+        nc.scalar.activation(out=warm2[:], in_=warm[:], func=ACT.Exp)
+        nc.vector.memset(brow[:], 0.0)
+        nc.vector.memset(bvrow[:], 0.0)
+        nc.vector.memset(halves[:], 0.5)
+        nc.scalar.dma_start(out=brow[0:8, :], in_=bq.rearrange("(i p) -> i p", p=P))
+        nc.scalar.dma_start(out=bvrow[0:1, :], in_=bv.rearrange("(o h) -> o h", o=1))
+
+        x_raw = const.tile([P, B * D], BF16, name="x_raw")
+        x_raw3 = x_raw[:].rearrange("p (b k) -> p b k", b=B)
+        x_t = x.rearrange("b t k -> t b k")
+        w_dram = {"k": Wk, "v": Wv, "q": Wq}
+        w_raw = {}
+
+        def load_x(j):
+            nc.sync.dma_start(out=x_raw3[:, 2 * j:2 * j + 2, :], in_=x_t[:, 2 * j:2 * j + 2, :])
+
+        def load_w(w, c):
+            t = const.tile([P, 2 * D], BF16, name="wraw_%s%d" % (w, c))
+            nc.sync.dma_start(
+                out=t[:].rearrange("p (i k) -> p i k", i=2),
+                in_=w_dram[w][c * CH:(c + 1) * CH, :].rearrange("(i p) k -> p i k", p=P),
+            )
+            w_raw[(w, c)] = t
+
+        load_x(0)
+        load_x(1)
+        load_w("k", 0)
+        load_w("v", 0)
+        load_x(2)
+        load_x(3)
+        load_w("q", 0)
+        for c in range(1, NCH):
+            for w in ("k", "v", "q"):
+                load_w(w, c)
+
+        nc.vector.tensor_copy(out=identb[:], in_=ident[:])
+
+        def bias_stage():
+            bt = trp.tile([P, P], BF16, name="bt", tag="tr")
+            nc.tensor.transpose(out=bt[:], in_=brow[:], identity=identb[:])
+            nc.vector.tensor_scalar_mul(out=bqh[:], in0=bt[:, 0:8], scalar1=0.5)
+            for hh in range(2):
+                bb_ps = otp.tile([P, 512], F32, name="bb_ps", tag="ot")
+                nc.tensor.matmul(out=bb_ps[:], lhsT=halves[:], rhs=bvrow[:, hh * 512:(hh + 1) * 512],
+                                 start=True, stop=True)
+                nc.vector.tensor_copy(out=bvh[:, hh * 512:(hh + 1) * 512], in_=bb_ps[:])
+
+        xw = x_raw[:].bitcast(F32)
+        gx = [const.tile([P, 2048], F32, name="gx%d" % h, align_bytes=64) for h in range(2)]
+        xc = [const.tile([P, 1024], U32, name="xc%d" % h, align_bytes=64) for h in range(2)]
+        xs = [const.tile([P, 1024], U8, name="xs%d" % h, align_bytes=64) for h in range(2)]
+
+        def transpose_bank(words, first_col):
+            bank = trp.tile([P, 4, P], F32, name="trb", tag="tr")
+            for j in range(4):
+                nc.tensor.transpose(out=bank[:, j, :],
+                                    in_=words[:, first_col + j * P:first_col + (j + 1) * P],
+                                    identity=ident[:])
+            return bank[:].rearrange("p (g u) r -> p g r u", g=2, u=2)
+
+        def trx(b):
+            src = transpose_bank(xw, b * 512)
+            dst = gx[b // 4][:].rearrange("p (g b r u) -> p g b r u", g=2, b=4, r=P, u=2)[:, :, b % 4, :, :]
+            if b % 2 == 0:
+                nc.vector.tensor_copy(out=dst, in_=src)
+            else:
+                nc.scalar.copy(out=dst, in_=src)
+            if b % 4 == 3:
+                h = b // 4
+                nc.vector.quantize_mx(out=xc[h][:].bitcast(FP8X4), scales=xs[h][:], in_=gx[h][:].bitcast(BF16))
+
+        wc = {}
+        ws = {}
+
+        def trw_bank(w, c, i, gw, on_vector=False):
+            src = transpose_bank(w_raw[(w, c)][:].bitcast(F32), i * 512)
+            dst = gw[:].rearrange("p (g i r u) -> p g i r u", g=2, i=2, r=P, u=2)[:, :, i, :, :]
+            if on_vector:
+                nc.vector.tensor_copy(out=dst, in_=src)
+            else:
+                nc.scalar.copy(out=dst, in_=src)
+
+        def trw_quant(w, c, gw):
+            codes = const.tile([P, 512], U32, name="wc_%s%d" % (w, c), align_bytes=64)
+            scales = const.tile([P, 512], U8, name="ws_%s%d" % (w, c), align_bytes=64)
+            nc.vector.quantize_mx(out=codes[:].bitcast(FP8X4), scales=scales[:], in_=gw[:].bitcast(BF16))
+            wc[(w, c)] = codes
+            ws[(w, c)] = scales
+
+        def new_gw():
+            gw = gwp.tile([P, 1024], F32, name="gw", tag="gw", align_bytes=64)
+            return gw
+
+        def kv_bank(w, c, pb):
+            bank = mxp.tile([P, 2, CH], F32, name="kvb", tag="mx")
+            for bb in range(2):
+                b = 2 * pb + bb
+                h = b // 4
+                for g in range(2):
+                    xcols = slice(g * 512 + (b % 4) * P, g * 512 + (b % 4) * P + P)
+                    wcols = slice(g * CH, (g + 1) * CH)
+                    nc.tensor.matmul_mx(out=bank[:, bb, :],
+                                        lhsT=xc[h][:, xcols].bitcast(FP8X4), lhsT_scale=xs[h][:, xcols],
+                                        rhs=wc[(w, c)][:, wcols].bitcast(FP8X4), rhs_scale=ws[(w, c)][:, wcols],
+                                        start=(g == 0), stop=(g == 1))
+            return bank
+
+        def chain(eng, acc, tiles, pb, nm):
+            if pb == 1:
+                acc = accp.tile([P, 2, CH], F32, name=nm, tag=nm)
+                eng.tensor_tensor(out=acc[:], in0=tiles[0][:], in1=tiles[1][:], op=ALU.add)
+            elif pb > 1:
+                eng.tensor_tensor(out=acc[:], in0=acc[:], in1=tiles[pb][:], op=ALU.add)
+            return acc
+
+        def kv_stage(c, order, mid):
+            numer = {}
+            prod = {}
+            acc_n = None
+            acc_p = None
+            p_eng = nc.gpsimd if (PSUM_ON_G and c + 1 < NCH) else nc.vector
+            for step, (w, pb) in enumerate(order):
+                if step == 4 and mid is not None:
+                    mid()
+                bank = kv_bank(w, c, pb)
+                if w == "k":
+                    n = nump.tile([P, 2, CH], F32, name="numer", tag="numer")
+                    nc.scalar.activation(out=n[:], in_=bank[:], func=ACT.Exp)
+                    numer[pb] = n
+                    acc_n = chain(nc.gpsimd, acc_n, numer, pb, "acc_n")
+                else:
+                    pr = prodp.tile([P, 2, CH], F32, name="prod", tag="prod")
+                    nc.vector.tensor_tensor(out=pr[:], in0=bank[:], in1=numer[pb][:], op=ALU.mult)
+                    prod[pb] = pr
+                    acc_p = chain(p_eng, acc_p, prod, pb, "acc_p")
+                if w == "k" and pb == 3:
+                    den = accp.tile([P, CH], F32, name="den", tag="den")
+                    nc.gpsimd.tensor_tensor(out=den[:], in0=acc_n[:, 0, :], in1=acc_n[:, 1, :], op=ALU.add)
+            sp = accp.tile([P, CH], F32, name="sp", tag="sp")
+            p_eng.tensor_tensor(out=sp[:], in0=acc_p[:, 0, :], in1=acc_p[:, 1, :], op=ALU.add)
+            return den, sp
+
+        def weighted(c, den, sp):
+            rden = accp.tile([P, CH], F32, name="rden", tag="rden")
+            nc.vector.reciprocal(out=rden[:], in_=den[:])
+            t1 = accp.tile([P, CH], F32, name="t1", tag="t1")
+            nc.vector.scalar_tensor_tensor(out=t1[:], in0=sp[:], scalar=0.5, in1=rden[:],
+                                           op0=ALU.mult, op1=ALU.mult)
+            wh = accp.tile([P, CH], F32, name="wh", tag="wh")
+            nc.vector.tensor_tensor(out=wh[:], in0=t1[:], in1=bvh[:, c * CH:(c + 1) * CH], op=ALU.add)
+            return wh
+
+        def qt_stage(c):
+            th = {}
+            for i in range(2):
+                for h in range(2):
+                    qb = mxp.tile([P, 512], F32, name="qb", tag="mx")
+                    for g in range(2):
+                        wcols = slice(g * CH + i * P, g * CH + (i + 1) * P)
+                        xcols = slice(g * 512, (g + 1) * 512)
+                        nc.tensor.matmul_mx(out=qb[:],
+                                            lhsT=wc[("q", c)][:, wcols].bitcast(FP8X4),
+                                            lhsT_scale=ws[("q", c)][:, wcols],
+                                            rhs=xc[h][:, xcols].bitcast(FP8X4), rhs_scale=xs[h][:, xcols],
+                                            start=(g == 0), stop=(g == 1))
+                    t = thp.tile([P, 512], F32, name="th", tag="th")
+                    nc.scalar.activation(out=t[:], in_=qb[:], func=ACT.Tanh,
+                                         bias=bqh[:, 2 * c + i:2 * c + i + 1], scale=0.5)
+                    th[(i, h)] = t
+            return th
+
+        def ot_bank(c, pb, th, wh):
+            ob = otp.tile([P, 2, CH], F32, name="ob", tag="ot")
+            for bb in range(2):
+                b = 2 * pb + bb
+                for i in range(2):
+                    nc.tensor.transpose(out=ob[:, bb, i * P:(i + 1) * P],
+                                        in_=th[(i, b // 4)][:, (b % 4) * P:(b % 4 + 1) * P],
+                                        identity=ident[:])
+            o = outp.tile([P, 2, CH], F32, name="o", tag="o")
+            nc.vector.scalar_tensor_tensor(out=o[:], in0=ob[:], scalar=1.0,
+                                           in1=wh[:].unsqueeze(1).to_broadcast([P, 2, CH]),
+                                           op0=ALU.add, op1=ALU.mult)
+            nc.sync.dma_start(out=out[2 * pb:2 * pb + 2, :, c * CH:(c + 1) * CH].rearrange("b t h -> t b h"),
+                              in_=o[:])
+
+        def head_w(w):
+            gw = new_gw()
+            trw_bank(w, 0, 0, gw, on_vector=True)
+            trw_bank(w, 0, 1, gw)
+            trw_quant(w, 0, gw)
+
+        def head_mid():
+            for b in range(4, 8):
+                trx(b)
+            bias_stage()
+            head_w("q")
+
+        for b in range(4):
+            trx(b)
+        head_w("k")
+        head_w("v")
+
+        lead = (("k", 0), ("k", 1), ("v", 0), ("k", 2), ("v", 1), ("k", 3), ("v", 2), ("v", 3))
+        halves_first = (("k", 0), ("k", 1), ("v", 0), ("v", 1), ("k", 2), ("k", 3), ("v", 2), ("v", 3))
+        for c in range(NCH):
+            if c == 0:
+                den, sp = kv_stage(c, halves_first, head_mid)
+            else:
+                den, sp = kv_stage(c, lead, None)
+            th = qt_stage(c)
+            wh = weighted(c, den, sp)
+            if c + 1 < NCH:
+                gk = new_gw()
+                trw_bank("k", c + 1, 0, gk)
+                trw_bank("k", c + 1, 1, gk)
+                ot_bank(c, 0, th, wh)
+                trw_quant("k", c + 1, gk)
+                gv = new_gw()
+                trw_bank("v", c + 1, 0, gv)
+                ot_bank(c, 1, th, wh)
+                trw_bank("v", c + 1, 1, gv)
+                ot_bank(c, 2, th, wh)
+                trw_quant("v", c + 1, gv)
+                gq = new_gw()
+                trw_bank("q", c + 1, 0, gq)
+                ot_bank(c, 3, th, wh)
+                trw_bank("q", c + 1, 1, gq)
+                trw_quant("q", c + 1, gq)
+            else:
+                for pb in range(4):
+                    ot_bank(c, pb, th, wh)

@@ -28,14 +28,15 @@ def tile_aftattention_kernel(tc, x, Wq, bq, Wk, bk, Wv, bv, wbias, out):
     with ExitStack() as ctx:
         const = ctx.enter_context(tc.tile_pool(name="const", bufs=1))
         gwp = ctx.enter_context(tc.tile_pool(name="gwp", bufs=4))
-        nump = ctx.enter_context(tc.tile_pool(name="nump", bufs=6))
+        nump = ctx.enter_context(tc.tile_pool(name="nump", bufs=8))
         prodp = ctx.enter_context(tc.tile_pool(name="prodp", bufs=6))
         accp = ctx.enter_context(tc.tile_pool(name="accp", bufs=2))
-        thp = ctx.enter_context(tc.tile_pool(name="thp", bufs=8))
+        thp = ctx.enter_context(tc.tile_pool(name="thp", bufs=12))
         outp = ctx.enter_context(tc.tile_pool(name="outp", bufs=4))
-        trp = ctx.enter_context(tc.psum_pool(name="trp", bufs=3))
-        mxp = ctx.enter_context(tc.psum_pool(name="mxp", bufs=3))
+        trp = ctx.enter_context(tc.psum_pool(name="trp", bufs=2))
         otp = ctx.enter_context(tc.psum_pool(name="otp", bufs=2))
+        mxp = ctx.enter_context(tc.psum_pool(name="mxp", bufs=4))
+        tpools = {"tr": trp, "ot": otp}
         if PINNED:
             ctx.enter_context(tc.manual_schedule())
 
@@ -75,9 +76,9 @@ def tile_aftattention_kernel(tc, x, Wq, bq, Wk, bk, Wv, bv, wbias, out):
             w_raw[(w, c)] = t
 
         load_x(0)
-        load_x(1)
         load_w("k", 0)
         load_w("v", 0)
+        load_x(1)
         load_x(2)
         load_x(3)
         load_w("q", 0)
@@ -102,46 +103,51 @@ def tile_aftattention_kernel(tc, x, Wq, bq, Wk, bk, Wv, bv, wbias, out):
         xc = [const.tile([P, 1024], U32, name="xc%d" % h, align_bytes=64) for h in range(2)]
         xs = [const.tile([P, 1024], U8, name="xs%d" % h, align_bytes=64) for h in range(2)]
 
-        def transpose_bank(words, first_col):
-            bank = trp.tile([P, 4, P], F32, name="trb", tag="tr")
+        def transpose_bank(words, first_col, tag):
+            bank = tpools[tag].tile([P, 4, P], F32, name="trb", tag=tag)
             for j in range(4):
                 nc.tensor.transpose(out=bank[:, j, :],
                                     in_=words[:, first_col + j * P:first_col + (j + 1) * P],
                                     identity=ident[:])
             return bank[:].rearrange("p (g u) r -> p g r u", g=2, u=2)
 
-        def trx(b):
-            src = transpose_bank(xw, b * 512)
-            dst = gx[b // 4][:].rearrange("p (g b r u) -> p g b r u", g=2, b=4, r=P, u=2)[:, :, b % 4, :, :]
-            if b % 2 == 0:
+        def evac(eng, dst, src):
+            if eng == "V":
                 nc.vector.tensor_copy(out=dst, in_=src)
             else:
                 nc.scalar.copy(out=dst, in_=src)
-            if b % 4 == 3:
-                h = b // 4
-                nc.vector.quantize_mx(out=xc[h][:].bitcast(FP8X4), scales=xs[h][:], in_=gx[h][:].bitcast(BF16))
+
+        def trx(b, tag, eng):
+            src = transpose_bank(xw, b * 512, tag)
+            dst = gx[b // 4][:].rearrange("p (g b r u) -> p g b r u", g=2, b=4, r=P, u=2)[:, :, b % 4, :, :]
+            evac(eng, dst, src)
+
+        def qx(pb):
+            h = pb // 2
+            for g in range(2):
+                w0 = g * 512 + (pb % 2) * 256
+                nc.vector.quantize_mx(out=xc[h][:, w0:w0 + 256].bitcast(FP8X4), scales=xs[h][:, w0:w0 + 256],
+                                      in_=gx[h][:, 2 * w0:2 * w0 + 512].bitcast(BF16))
 
         wc = {}
         ws = {}
+        gws = {}
 
-        def trw_bank(w, c, i, gw, on_vector=False):
-            src = transpose_bank(w_raw[(w, c)][:].bitcast(F32), i * 512)
-            dst = gw[:].rearrange("p (g i r u) -> p g i r u", g=2, i=2, r=P, u=2)[:, :, i, :, :]
-            if on_vector:
-                nc.vector.tensor_copy(out=dst, in_=src)
-            else:
-                nc.scalar.copy(out=dst, in_=src)
+        def trw(w, c, i, eng="S", tag="tr"):
+            if i == 0:
+                gw_new = gwp.tile([P, 1024], F32, name="gw", tag="gw", align_bytes=64)
+                gws[(w, c)] = gw_new
+            src = transpose_bank(w_raw[(w, c)][:].bitcast(F32), i * 512, tag)
+            dst = gws[(w, c)][:].rearrange("p (g i r u) -> p g i r u", g=2, i=2, r=P, u=2)[:, :, i, :, :]
+            evac(eng, dst, src)
 
-        def trw_quant(w, c, gw):
+        def tq(w, c):
             codes = const.tile([P, 512], U32, name="wc_%s%d" % (w, c), align_bytes=64)
             scales = const.tile([P, 512], U8, name="ws_%s%d" % (w, c), align_bytes=64)
-            nc.vector.quantize_mx(out=codes[:].bitcast(FP8X4), scales=scales[:], in_=gw[:].bitcast(BF16))
+            nc.vector.quantize_mx(out=codes[:].bitcast(FP8X4), scales=scales[:],
+                                  in_=gws[(w, c)][:].bitcast(BF16))
             wc[(w, c)] = codes
             ws[(w, c)] = scales
-
-        def new_gw():
-            gw = gwp.tile([P, 1024], F32, name="gw", tag="gw", align_bytes=64)
-            return gw
 
         def kv_bank(w, c, pb):
             bank = mxp.tile([P, 2, CH], F32, name="kvb", tag="mx")
@@ -157,128 +163,162 @@ def tile_aftattention_kernel(tc, x, Wq, bq, Wk, bk, Wv, bv, wbias, out):
                                         start=(g == 0), stop=(g == 1))
             return bank
 
-        def chain(eng, acc, tiles, pb, nm):
+        st = {}
+
+        def chain(eng, c, key, tiles, pb):
             if pb == 1:
-                acc = accp.tile([P, 2, CH], F32, name=nm, tag=nm)
+                acc = accp.tile([P, 2, CH], F32, name=key, tag=key)
+                st[(key, c)] = acc
                 eng.tensor_tensor(out=acc[:], in0=tiles[0][:], in1=tiles[1][:], op=ALU.add)
             elif pb > 1:
+                acc = st[(key, c)]
                 eng.tensor_tensor(out=acc[:], in0=acc[:], in1=tiles[pb][:], op=ALU.add)
-            return acc
+            if pb == 3:
+                acc = st[(key, c)]
+                tot = accp.tile([P, CH], F32, name=key + "_t", tag=key + "_t")
+                eng.tensor_tensor(out=tot[:], in0=acc[:, 0, :], in1=acc[:, 1, :], op=ALU.add)
+                st[(key + "_t", c)] = tot
 
-        def kv_stage(c, order, mid):
-            numer = {}
-            prod = {}
-            acc_n = None
-            acc_p = None
-            p_eng = nc.gpsimd if (PSUM_ON_G and c + 1 < NCH) else nc.vector
-            for step, (w, pb) in enumerate(order):
-                if step == 4 and mid is not None:
-                    mid()
-                bank = kv_bank(w, c, pb)
-                if w == "k":
-                    n = nump.tile([P, 2, CH], F32, name="numer", tag="numer")
-                    nc.scalar.activation(out=n[:], in_=bank[:], func=ACT.Exp)
-                    numer[pb] = n
-                    acc_n = chain(nc.gpsimd, acc_n, numer, pb, "acc_n")
-                else:
-                    pr = prodp.tile([P, 2, CH], F32, name="prod", tag="prod")
-                    nc.vector.tensor_tensor(out=pr[:], in0=bank[:], in1=numer[pb][:], op=ALU.mult)
-                    prod[pb] = pr
-                    acc_p = chain(p_eng, acc_p, prod, pb, "acc_p")
-                if w == "k" and pb == 3:
-                    den = accp.tile([P, CH], F32, name="den", tag="den")
-                    nc.gpsimd.tensor_tensor(out=den[:], in0=acc_n[:, 0, :], in1=acc_n[:, 1, :], op=ALU.add)
-            sp = accp.tile([P, CH], F32, name="sp", tag="sp")
-            p_eng.tensor_tensor(out=sp[:], in0=acc_p[:, 0, :], in1=acc_p[:, 1, :], op=ALU.add)
-            return den, sp
+        def kb(c, pb):
+            bank = kv_bank("k", c, pb)
+            n = nump.tile([P, 2, CH], F32, name="numer", tag="numer")
+            nc.scalar.activation(out=n[:], in_=bank[:], func=ACT.Exp)
+            if pb == 0:
+                st[("numer", c)] = {}
+            st[("numer", c)][pb] = n
+            chain(nc.gpsimd, c, "acc_n", st[("numer", c)], pb)
 
-        def weighted(c, den, sp):
+        def vb(c, pb):
+            bank = kv_bank("v", c, pb)
+            pr = prodp.tile([P, 2, CH], F32, name="prod", tag="prod")
+            nc.vector.tensor_tensor(out=pr[:], in0=bank[:], in1=st[("numer", c)][pb][:], op=ALU.mult)
+            if pb == 0:
+                st[("prod", c)] = {}
+            st[("prod", c)][pb] = pr
+            p_eng = nc.gpsimd if PSUM_ON_G else nc.vector
+            chain(p_eng, c, "acc_p", st[("prod", c)], pb)
+
+        def qb(c, i, h):
+            bank = mxp.tile([P, 512], F32, name="qbank", tag="mx")
+            for g in range(2):
+                wcols = slice(g * CH + i * P, g * CH + (i + 1) * P)
+                xcols = slice(g * 512, (g + 1) * 512)
+                nc.tensor.matmul_mx(out=bank[:],
+                                    lhsT=wc[("q", c)][:, wcols].bitcast(FP8X4), lhsT_scale=ws[("q", c)][:, wcols],
+                                    rhs=xc[h][:, xcols].bitcast(FP8X4), rhs_scale=xs[h][:, xcols],
+                                    start=(g == 0), stop=(g == 1))
+            t = thp.tile([P, 512], F32, name="th", tag="th")
+            nc.scalar.activation(out=t[:], in_=bank[:], func=ACT.Tanh,
+                                 bias=bqh[:, 2 * c + i:2 * c + i + 1], scale=0.5)
+            st[("th", c, i, h)] = t
+
+        def q4(c):
+            for i, h in ((0, 0), (1, 0), (0, 1), (1, 1)):
+                qb(c, i, h)
+
+        def recip(c):
             rden = accp.tile([P, CH], F32, name="rden", tag="rden")
-            nc.vector.reciprocal(out=rden[:], in_=den[:])
+            nc.vector.reciprocal(out=rden[:], in_=st[("acc_n_t", c)][:])
+            st[("rden", c)] = rden
+
+        def wgt(c):
             t1 = accp.tile([P, CH], F32, name="t1", tag="t1")
-            nc.vector.scalar_tensor_tensor(out=t1[:], in0=sp[:], scalar=0.5, in1=rden[:],
-                                           op0=ALU.mult, op1=ALU.mult)
+            nc.vector.scalar_tensor_tensor(out=t1[:], in0=st[("acc_p_t", c)][:], scalar=0.5,
+                                           in1=st[("rden", c)][:], op0=ALU.mult, op1=ALU.mult)
             wh = accp.tile([P, CH], F32, name="wh", tag="wh")
             nc.vector.tensor_tensor(out=wh[:], in0=t1[:], in1=bvh[:, c * CH:(c + 1) * CH], op=ALU.add)
-            return wh
+            st[("wh", c)] = wh
 
-        def qt_stage(c):
-            th = {}
-            for i in range(2):
-                for h in range(2):
-                    qb = mxp.tile([P, 512], F32, name="qb", tag="mx")
-                    for g in range(2):
-                        wcols = slice(g * CH + i * P, g * CH + (i + 1) * P)
-                        xcols = slice(g * 512, (g + 1) * 512)
-                        nc.tensor.matmul_mx(out=qb[:],
-                                            lhsT=wc[("q", c)][:, wcols].bitcast(FP8X4),
-                                            lhsT_scale=ws[("q", c)][:, wcols],
-                                            rhs=xc[h][:, xcols].bitcast(FP8X4), rhs_scale=xs[h][:, xcols],
-                                            start=(g == 0), stop=(g == 1))
-                    t = thp.tile([P, 512], F32, name="th", tag="th")
-                    nc.scalar.activation(out=t[:], in_=qb[:], func=ACT.Tanh,
-                                         bias=bqh[:, 2 * c + i:2 * c + i + 1], scale=0.5)
-                    th[(i, h)] = t
-            return th
-
-        def ot_bank(c, pb, th, wh):
-            ob = otp.tile([P, 2, CH], F32, name="ob", tag="ot")
+        def ot(c, pb, tag="ot"):
+            ob = tpools[tag].tile([P, 2, CH], F32, name="ob", tag=tag)
             for bb in range(2):
                 b = 2 * pb + bb
                 for i in range(2):
                     nc.tensor.transpose(out=ob[:, bb, i * P:(i + 1) * P],
-                                        in_=th[(i, b // 4)][:, (b % 4) * P:(b % 4 + 1) * P],
+                                        in_=st[("th", c, i, b // 4)][:, (b % 4) * P:(b % 4 + 1) * P],
                                         identity=ident[:])
             o = outp.tile([P, 2, CH], F32, name="o", tag="o")
             nc.vector.scalar_tensor_tensor(out=o[:], in0=ob[:], scalar=1.0,
-                                           in1=wh[:].unsqueeze(1).to_broadcast([P, 2, CH]),
+                                           in1=st[("wh", c)][:].unsqueeze(1).to_broadcast([P, 2, CH]),
                                            op0=ALU.add, op1=ALU.mult)
             nc.sync.dma_start(out=out[2 * pb:2 * pb + 2, :, c * CH:(c + 1) * CH].rearrange("b t h -> t b h"),
                               in_=o[:])
 
-        def head_w(w):
-            gw = new_gw()
-            trw_bank(w, 0, 0, gw, on_vector=True)
-            trw_bank(w, 0, 1, gw)
-            trw_quant(w, 0, gw)
+        trx(0, "tr", "V")
+        trx(1, "tr", "S")
+        qx(0)
+        trw("k", 0, 0, "V", "ot")
+        trw("k", 0, 1, "S", "ot")
+        tq("k", 0)
+        trw("v", 0, 0, "V")
+        trw("v", 0, 1, "S")
+        tq("v", 0)
+        trx(2, "ot", "V")
+        trx(3, "ot", "S")
+        qx(1)
+        kb(0, 0)
+        vb(0, 0)
+        trx(4, "tr", "V")
+        trx(5, "tr", "S")
+        qx(2)
+        kb(0, 1)
+        vb(0, 1)
+        trx(6, "ot", "V")
+        trx(7, "ot", "S")
+        qx(3)
+        kb(0, 2)
+        vb(0, 2)
+        trw("q", 0, 0, "V")
+        trw("q", 0, 1, "S")
+        tq("q", 0)
+        bias_stage()
+        kb(0, 3)
+        vb(0, 3)
+        trw("k", 1, 0, "V", "ot")
+        trw("k", 1, 1, "S", "ot")
+        tq("k", 1)
+        trw("v", 1, 0, "V")
+        trw("v", 1, 1)
+        tq("v", 1)
+        q4(0)
+        recip(0)
+        trw("q", 1, 0, "S", "ot")
+        trw("q", 1, 1, "S", "ot")
+        tq("q", 1)
 
-        def head_mid():
-            for b in range(4, 8):
-                trx(b)
-            bias_stage()
-            head_w("q")
-
-        for b in range(4):
-            trx(b)
-        head_w("k")
-        head_w("v")
-
-        lead = (("k", 0), ("k", 1), ("v", 0), ("k", 2), ("v", 1), ("k", 3), ("v", 2), ("v", 3))
-        halves_first = (("k", 0), ("k", 1), ("v", 0), ("v", 1), ("k", 2), ("k", 3), ("v", 2), ("v", 3))
-        for c in range(NCH):
-            if c == 0:
-                den, sp = kv_stage(c, halves_first, head_mid)
-            else:
-                den, sp = kv_stage(c, lead, None)
-            th = qt_stage(c)
-            wh = weighted(c, den, sp)
-            if c + 1 < NCH:
-                gk = new_gw()
-                trw_bank("k", c + 1, 0, gk)
-                trw_bank("k", c + 1, 1, gk)
-                ot_bank(c, 0, th, wh)
-                trw_quant("k", c + 1, gk)
-                gv = new_gw()
-                trw_bank("v", c + 1, 0, gv)
-                ot_bank(c, 1, th, wh)
-                trw_bank("v", c + 1, 1, gv)
-                ot_bank(c, 2, th, wh)
-                trw_quant("v", c + 1, gv)
-                gq = new_gw()
-                trw_bank("q", c + 1, 0, gq)
-                ot_bank(c, 3, th, wh)
-                trw_bank("q", c + 1, 1, gq)
-                trw_quant("q", c + 1, gq)
-            else:
-                for pb in range(4):
-                    ot_bank(c, pb, th, wh)
+        for c in range(1, NCH):
+            more = c + 1 < NCH
+            kb(c, 0)
+            kb(c, 1)
+            vb(c, 0)
+            kb(c, 2)
+            wgt(c - 1)
+            if more:
+                trw("k", c + 1, 0)
+                trw("k", c + 1, 1)
+            ot(c - 1, 0)
+            ot(c - 1, 1)
+            if more:
+                tq("k", c + 1)
+            kb(c, 3)
+            vb(c, 1)
+            vb(c, 2)
+            vb(c, 3)
+            if more:
+                trw("v", c + 1, 0)
+                trw("v", c + 1, 1)
+            ot(c - 1, 2)
+            ot(c - 1, 3)
+            if more:
+                tq("v", c + 1)
+            q4(c)
+            recip(c)
+            if more:
+                trw("q", c + 1, 0)
+                trw("q", c + 1, 1)
+                tq("q", c + 1)
+        wgt(NCH - 1)
+        ot(NCH - 1, 0)
+        ot(NCH - 1, 1)
+        ot(NCH - 1, 2, "tr")
+        ot(NCH - 1, 3, "tr")

@@ -20,7 +20,7 @@ H = 1024
 CH = 256
 NCH = H // CH
 PINNED = True
-PSUM_ON_G = True
+PSUM_ON_G = False
 
 
 def tile_aftattention_kernel(tc, x, Wq, bq, Wk, bk, Wv, bv, wbias, out):

@@ -19,8 +19,8 @@ D = 1024
 H = 1024
 CH = 256
 NCH = H // CH
-PINNED = True
-PSUM_ON_G = False
+PINNED = False
+PSUM_ON_G = True
 
 
 def tile_aftattention_kernel(tc, x, Wq, bq, Wk, bk, Wv, bv, wbias, out):

@@ -19,7 +19,7 @@ D = 1024
 H = 1024
 CH = 256
 NCH = H // CH
-PINNED = False
+PINNED = True
 PSUM_ON_G = True
 
 
@@ -44,19 +44,14 @@ def tile_aftattention_kernel(tc, x, Wq, bq, Wk, bk, Wv, bv, wbias, out):
         make_identity(nc, ident[:])
         identb = const.tile([P, P], BF16, name="identb")
         brow = const.tile([P, P], BF16, name="brow")
-        bvrow = const.tile([P, H], BF16, name="bvrow")
-        halves = const.tile([P, P], BF16, name="halves")
+        bvb = const.tile([P, H], BF16, name="bvb")
         warm = const.tile([P, 1], F32, name="warm")
         warm2 = const.tile([P, 1], F32, name="warm2")
         bqh = const.tile([P, 8], F32, name="bqh")
-        bvh = const.tile([P, H], F32, name="bvh")
         nc.vector.memset(warm[:], 0.0)
         nc.scalar.activation(out=warm2[:], in_=warm[:], func=ACT.Exp)
         nc.vector.memset(brow[:], 0.0)
-        nc.vector.memset(bvrow[:], 0.0)
-        nc.vector.memset(halves[:], 0.5)
         nc.scalar.dma_start(out=brow[0:8, :], in_=bq.rearrange("(i p) -> i p", p=P))
-        nc.scalar.dma_start(out=bvrow[0:1, :], in_=bv.rearrange("(o h) -> o h", o=1))
 
         x_raw = const.tile([P, B * D], BF16, name="x_raw")
         x_raw3 = x_raw[:].rearrange("p (b k) -> p b k", b=B)
@@ -75,7 +70,8 @@ def tile_aftattention_kernel(tc, x, Wq, bq, Wk, bk, Wv, bv, wbias, out):
             )
             w_raw[(w, c)] = t
 
-        load_x(0)
+        nc.sync.dma_start(out=x_raw3[:, 0:1, :], in_=x_t[:, 0:1, :])
+        nc.sync.dma_start(out=x_raw3[:, 1:2, :], in_=x_t[:, 1:2, :])
         load_w("k", 0)
         load_w("v", 0)
         load_x(1)
@@ -85,6 +81,8 @@ def tile_aftattention_kernel(tc, x, Wq, bq, Wk, bk, Wv, bv, wbias, out):
         for c in range(1, NCH):
             for w in ("k", "v", "q"):
                 load_w(w, c)
+            if c == 1:
+                nc.sync.dma_start(out=bvb[:], in_=bv.partition_broadcast(P))
 
         nc.vector.tensor_copy(out=identb[:], in_=ident[:])
 
@@ -92,11 +90,6 @@ def tile_aftattention_kernel(tc, x, Wq, bq, Wk, bk, Wv, bv, wbias, out):
             bt = trp.tile([P, P], BF16, name="bt", tag="tr")
             nc.tensor.transpose(out=bt[:], in_=brow[:], identity=identb[:])
             nc.vector.tensor_scalar_mul(out=bqh[:], in0=bt[:, 0:8], scalar1=0.5)
-            for hh in range(2):
-                bb_ps = otp.tile([P, 512], F32, name="bb_ps", tag="ot")
-                nc.tensor.matmul(out=bb_ps[:], lhsT=halves[:], rhs=bvrow[:, hh * 512:(hh + 1) * 512],
-                                 start=True, stop=True)
-                nc.vector.tensor_copy(out=bvh[:, hh * 512:(hh + 1) * 512], in_=bb_ps[:])
 
         xw = x_raw[:].bitcast(F32)
         gx = [const.tile([P, 2048], F32, name="gx%d" % h, align_bytes=64) for h in range(2)]
@@ -226,7 +219,8 @@ def tile_aftattention_kernel(tc, x, Wq, bq, Wk, bk, Wv, bv, wbias, out):
             nc.vector.scalar_tensor_tensor(out=t1[:], in0=st[("acc_p_t", c)][:], scalar=0.5,
                                            in1=st[("rden", c)][:], op0=ALU.mult, op1=ALU.mult)
             wh = accp.tile([P, CH], F32, name="wh", tag="wh")
-            nc.vector.tensor_tensor(out=wh[:], in0=t1[:], in1=bvh[:, c * CH:(c + 1) * CH], op=ALU.add)
+            nc.vector.scalar_tensor_tensor(out=wh[:], in0=bvb[:, c * CH:(c + 1) * CH], scalar=0.5, in1=t1[:],
+                                           op0=ALU.mult, op1=ALU.add)
             st[("wh", c)] = wh
 
         def ot(c, pb, tag="ot"):

from contextlib import ExitStack

import concourse.mybir as mybir
from concourse.masks import make_identity

FLOPS = 2 * 1024 * 1024 * 3072

F32 = mybir.dt.float32
BF16 = mybir.dt.bfloat16
U32 = mybir.dt.uint32
U8 = mybir.dt.uint8
FP8X4 = mybir.dt.float8_e4m3fn_x4
ACT = mybir.ActivationFunctionType
ALU = mybir.AluOpType

P = 128
B = 8
D = 1024
H = 1024
CH = 256
NCH = H // CH
PINNED = True
PSUM_ON_G = True


def tile_aftattention_kernel(tc, x, Wq, bq, Wk, bk, Wv, bv, wbias, out):
    nc = tc.nc
    with ExitStack() as ctx:
        const = ctx.enter_context(tc.tile_pool(name="const", bufs=1))
        gwp = ctx.enter_context(tc.tile_pool(name="gwp", bufs=4))
        nump = ctx.enter_context(tc.tile_pool(name="nump", bufs=8))
        prodp = ctx.enter_context(tc.tile_pool(name="prodp", bufs=6))
        accp = ctx.enter_context(tc.tile_pool(name="accp", bufs=2))
        thp = ctx.enter_context(tc.tile_pool(name="thp", bufs=12))
        outp = ctx.enter_context(tc.tile_pool(name="outp", bufs=4))
        trp = ctx.enter_context(tc.psum_pool(name="trp", bufs=2))
        otp = ctx.enter_context(tc.psum_pool(name="otp", bufs=2))
        mxp = ctx.enter_context(tc.psum_pool(name="mxp", bufs=4))
        tpools = {"tr": trp, "ot": otp}
        if PINNED:
            ctx.enter_context(tc.manual_schedule())

        ident = const.tile([P, P], F32, name="ident")
        make_identity(nc, ident[:])
        identb = const.tile([P, P], BF16, name="identb")
        brow = const.tile([P, P], BF16, name="brow")
        bvb = const.tile([P, H], BF16, name="bvb")
        warm = const.tile([P, 1], F32, name="warm")
        warm2 = const.tile([P, 1], F32, name="warm2")
        bqh = const.tile([P, 8], F32, name="bqh")
        nc.vector.memset(warm[:], 0.0)
        nc.scalar.activation(out=warm2[:], in_=warm[:], func=ACT.Exp)
        nc.vector.memset(brow[:], 0.0)
        nc.scalar.dma_start(out=brow[0:8, :], in_=bq.rearrange("(i p) -> i p", p=P))

        x_raw = const.tile([P, B * D], BF16, name="x_raw")
        x_raw3 = x_raw[:].rearrange("p (b k) -> p b k", b=B)
        x_t = x.rearrange("b t k -> t b k")
        w_dram = {"k": Wk, "v": Wv, "q": Wq}
        w_raw = {}

        def load_x(j):
            nc.sync.dma_start(out=x_raw3[:, 2 * j:2 * j + 2, :], in_=x_t[:, 2 * j:2 * j + 2, :])

        def load_w(w, c):
            t = const.tile([P, 2 * D], BF16, name="wraw_%s%d" % (w, c))
            nc.sync.dma_start(
                out=t[:].rearrange("p (i k) -> p i k", i=2),
                in_=w_dram[w][c * CH:(c + 1) * CH, :].rearrange("(i p) k -> p i k", p=P),
            )
            w_raw[(w, c)] = t

        nc.sync.dma_start(out=x_raw3[:, 0:1, :], in_=x_t[:, 0:1, :])
        nc.sync.dma_start(out=x_raw3[:, 1:2, :], in_=x_t[:, 1:2, :])
        load_w("k", 0)
        load_w("v", 0)
        load_x(1)
        load_x(2)
        load_x(3)
        load_w("q", 0)
        for c in range(1, NCH):
            for w in ("k", "v", "q"):
                load_w(w, c)
            if c == 1:
                nc.sync.dma_start(out=bvb[:], in_=bv.partition_broadcast(P))

        nc.vector.tensor_copy(out=identb[:], in_=ident[:])

        def bias_stage():
            bt = trp.tile([P, P], BF16, name="bt", tag="tr")
            nc.tensor.transpose(out=bt[:], in_=brow[:], identity=identb[:])
            nc.vector.tensor_scalar_mul(out=bqh[:], in0=bt[:, 0:8], scalar1=0.5)

        xw = x_raw[:].bitcast(F32)
        gx = [const.tile([P, 2048], F32, name="gx%d" % h, align_bytes=64) for h in range(2)]
        xc = [const.tile([P, 1024], U32, name="xc%d" % h, align_bytes=64) for h in range(2)]
        xs = [const.tile([P, 1024], U8, name="xs%d" % h, align_bytes=64) for h in range(2)]

        def transpose_bank(words, first_col, tag):
            bank = tpools[tag].tile([P, 4, P], F32, name="trb", tag=tag)
            for j in range(4):
                nc.tensor.transpose(out=bank[:, j, :],
                                    in_=words[:, first_col + j * P:first_col + (j + 1) * P],
                                    identity=ident[:])
            return bank[:].rearrange("p (g u) r -> p g r u", g=2, u=2)

        def evac(eng, dst, src):
            if eng == "V":
                nc.vector.tensor_copy(out=dst, in_=src)
            else:
                nc.scalar.copy(out=dst, in_=src)

        def trx(b, tag, eng):
            src = transpose_bank(xw, b * 512, tag)
            dst = gx[b // 4][:].rearrange("p (g b r u) -> p g b r u", g=2, b=4, r=P, u=2)[:, :, b % 4, :, :]
            evac(eng, dst, src)

        def qx(pb):
            h = pb // 2
            for g in range(2):
                w0 = g * 512 + (pb % 2) * 256
                nc.vector.quantize_mx(out=xc[h][:, w0:w0 + 256].bitcast(FP8X4), scales=xs[h][:, w0:w0 + 256],
                                      in_=gx[h][:, 2 * w0:2 * w0 + 512].bitcast(BF16))

        wc = {}
        ws = {}
        gws = {}

        def trw(w, c, i, eng="S", tag="tr"):
            if i == 0:
                gw_new = gwp.tile([P, 1024], F32, name="gw", tag="gw", align_bytes=64)
                gws[(w, c)] = gw_new
            src = transpose_bank(w_raw[(w, c)][:].bitcast(F32), i * 512, tag)
            dst = gws[(w, c)][:].rearrange("p (g i r u) -> p g i r u", g=2, i=2, r=P, u=2)[:, :, i, :, :]
            evac(eng, dst, src)

        def tq(w, c):
            codes = const.tile([P, 512], U32, name="wc_%s%d" % (w, c), align_bytes=64)
            scales = const.tile([P, 512], U8, name="ws_%s%d" % (w, c), align_bytes=64)
            nc.vector.quantize_mx(out=codes[:].bitcast(FP8X4), scales=scales[:],
                                  in_=gws[(w, c)][:].bitcast(BF16))
            wc[(w, c)] = codes
            ws[(w, c)] = scales

        def kv_bank(w, c, pb):
            bank = mxp.tile([P, 2, CH], F32, name="kvb", tag="mx")
            for bb in range(2):
                b = 2 * pb + bb
                h = b // 4
                for g in range(2):
                    xcols = slice(g * 512 + (b % 4) * P, g * 512 + (b % 4) * P + P)
                    wcols = slice(g * CH, (g + 1) * CH)
                    nc.tensor.matmul_mx(out=bank[:, bb, :],
                                        lhsT=xc[h][:, xcols].bitcast(FP8X4), lhsT_scale=xs[h][:, xcols],
                                        rhs=wc[(w, c)][:, wcols].bitcast(FP8X4), rhs_scale=ws[(w, c)][:, wcols],
                                        start=(g == 0), stop=(g == 1))
            return bank

        st = {}

        def chain(eng, c, key, tiles, pb):
            if pb == 1:
                acc = accp.tile([P, 2, CH], F32, name=key, tag=key)
                st[(key, c)] = acc
                eng.tensor_tensor(out=acc[:], in0=tiles[0][:], in1=tiles[1][:], op=ALU.add)
            elif pb > 1:
                acc = st[(key, c)]
                eng.tensor_tensor(out=acc[:], in0=acc[:], in1=tiles[pb][:], op=ALU.add)
            if pb == 3:
                acc = st[(key, c)]
                tot = accp.tile([P, CH], F32, name=key + "_t", tag=key + "_t")
                eng.tensor_tensor(out=tot[:], in0=acc[:, 0, :], in1=acc[:, 1, :], op=ALU.add)
                st[(key + "_t", c)] = tot

        def kb(c, pb):
            bank = kv_bank("k", c, pb)
            n = nump.tile([P, 2, CH], F32, name="numer", tag="numer")
            nc.scalar.activation(out=n[:], in_=bank[:], func=ACT.Exp)
            if pb == 0:
                st[("numer", c)] = {}
            st[("numer", c)][pb] = n
            chain(nc.gpsimd, c, "acc_n", st[("numer", c)], pb)

        def vb(c, pb):
            bank = kv_bank("v", c, pb)
            pr = prodp.tile([P, 2, CH], F32, name="prod", tag="prod")
            nc.vector.tensor_tensor(out=pr[:], in0=bank[:], in1=st[("numer", c)][pb][:], op=ALU.mult)
            if pb == 0:
                st[("prod", c)] = {}
            st[("prod", c)][pb] = pr
            p_eng = nc.gpsimd if PSUM_ON_G else nc.vector
            chain(p_eng, c, "acc_p", st[("prod", c)], pb)

        def qb(c, i, h):
            bank = mxp.tile([P, 512], F32, name="qbank", tag="mx")
            for g in range(2):
                wcols = slice(g * CH + i * P, g * CH + (i + 1) * P)
                xcols = slice(g * 512, (g + 1) * 512)
                nc.tensor.matmul_mx(out=bank[:],
                                    lhsT=wc[("q", c)][:, wcols].bitcast(FP8X4), lhsT_scale=ws[("q", c)][:, wcols],
                                    rhs=xc[h][:, xcols].bitcast(FP8X4), rhs_scale=xs[h][:, xcols],
                                    start=(g == 0), stop=(g == 1))
            t = thp.tile([P, 512], F32, name="th", tag="th")
            nc.scalar.activation(out=t[:], in_=bank[:], func=ACT.Tanh,
                                 bias=bqh[:, 2 * c + i:2 * c + i + 1], scale=0.5)
            st[("th", c, i, h)] = t

        def q4(c):
            for i, h in ((0, 0), (1, 0), (0, 1), (1, 1)):
                qb(c, i, h)

        def recip(c):
            rden = accp.tile([P, CH], F32, name="rden", tag="rden")
            nc.vector.reciprocal(out=rden[:], in_=st[("acc_n_t", c)][:])
            st[("rden", c)] = rden

        def wgt(c):
            t1 = accp.tile([P, CH], F32, name="t1", tag="t1")
            nc.vector.scalar_tensor_tensor(out=t1[:], in0=st[("acc_p_t", c)][:], scalar=0.5,
                                           in1=st[("rden", c)][:], op0=ALU.mult, op1=ALU.mult)
            wh = accp.tile([P, CH], F32, name="wh", tag="wh")
            nc.vector.scalar_tensor_tensor(out=wh[:], in0=bvb[:, c * CH:(c + 1) * CH], scalar=0.5, in1=t1[:],
                                           op0=ALU.mult, op1=ALU.add)
            st[("wh", c)] = wh

        def ot(c, pb, tag="ot"):
            ob = tpools[tag].tile([P, 2, CH], F32, name="ob", tag=tag)
            for bb in range(2):
                b = 2 * pb + bb
                for i in range(2):
                    nc.tensor.transpose(out=ob[:, bb, i * P:(i + 1) * P],
                                        in_=st[("th", c, i, b // 4)][:, (b % 4) * P:(b % 4 + 1) * P],
                                        identity=ident[:])
            o = outp.tile([P, 2, CH], F32, name="o", tag="o")
            nc.vector.scalar_tensor_tensor(out=o[:], in0=ob[:], scalar=1.0,
                                           in1=st[("wh", c)][:].unsqueeze(1).to_broadcast([P, 2, CH]),
                                           op0=ALU.add, op1=ALU.mult)
            nc.sync.dma_start(out=out[2 * pb:2 * pb + 2, :, c * CH:(c + 1) * CH].rearrange("b t h -> t b h"),
                              in_=o[:])

        trx(0, "tr", "V")
        trx(1, "tr", "S")
        qx(0)
        trw("k", 0, 0, "V", "ot")
        trw("k", 0, 1, "S", "ot")
        tq("k", 0)
        trw("v", 0, 0, "V")
        trw("v", 0, 1, "S")
        tq("v", 0)
        trx(2, "ot", "V")
        trx(3, "ot", "S")
        qx(1)
        kb(0, 0)
        vb(0, 0)
        trx(4, "tr", "V")
        trx(5, "tr", "S")
        qx(2)
        kb(0, 1)
        vb(0, 1)
        trx(6, "ot", "V")
        trx(7, "ot", "S")
        qx(3)
        kb(0, 2)
        vb(0, 2)
        trw("q", 0, 0, "V")
        trw("q", 0, 1, "S")
        tq("q", 0)
        bias_stage()
        kb(0, 3)
        vb(0, 3)
        trw("k", 1, 0, "V", "ot")
        trw("k", 1, 1, "S", "ot")
        tq("k", 1)
        trw("v", 1, 0, "V")
        trw("v", 1, 1)
        tq("v", 1)
        q4(0)
        recip(0)
        trw("q", 1, 0, "S", "ot")
        trw("q", 1, 1, "S", "ot")
        tq("q", 1)

        for c in range(1, NCH):
            more = c + 1 < NCH
            kb(c, 0)
            kb(c, 1)
            vb(c, 0)
            kb(c, 2)
            wgt(c - 1)
            if more:
                trw("k", c + 1, 0)
                trw("k", c + 1, 1)
            ot(c - 1, 0)
            ot(c - 1, 1)
            if more:
                tq("k", c + 1)
            kb(c, 3)
            vb(c, 1)
            vb(c, 2)
            vb(c, 3)
            if more:
                trw("v", c + 1, 0)
                trw("v", c + 1, 1)
            ot(c - 1, 2)
            ot(c - 1, 3)
            if more:
                tq("v", c + 1)
            q4(c)
            recip(c)
            if more:
                trw("q", c + 1, 0)
                trw("q", c + 1, 1)
                tq("q", c + 1)
        wgt(NCH - 1)
        ot(NCH - 1, 0)
        ot(NCH - 1, 1)
        ot(NCH - 1, 2, "tr")
        ot(NCH - 1, 3, "tr")
